import numpy as np
import ml_dtypes


def mxq(x, axis, fmt="e4m3"):
    dtype, down = {"e4m3": (ml_dtypes.float8_e4m3fn, 7), "e5m2": (ml_dtypes.float8_e5m2, 14)}[fmt]
    v = np.moveaxis(np.asarray(x, np.float32).astype(ml_dtypes.bfloat16).astype(np.float64), axis, -1)
    blocks = v.reshape(v.shape[:-1] + (-1, 32))
    amax = np.abs(blocks).max(-1, keepdims=True)
    byte = np.maximum(np.where(amax > 0, np.frexp(amax)[1] - 1 + 127, 0) - down, 1)
    scale = np.exp2(byte - 127.0)
    codes = (blocks / scale).astype(np.float32).astype(dtype).astype(np.float64)
    return np.moveaxis((codes * scale).reshape(v.shape), -1, axis)


WIDE = False


def mx_kscale(k):
    if not WIDE:
        return np.ones(k)
    levels = np.array([10, -10, 5, -5, 0])
    if k % 512:
        return np.exp2(np.random.permutation(np.resize(levels, k // 32))).repeat(32)
    a = np.empty((k // 512, 16))
    for p in range(k // 512):
        a[p, :8] = np.random.permutation(np.resize(levels, 8))
        for g in range(8):
            far = levels[np.abs(levels - a[p, g]) >= 10]
            a[p, g + 8] = far[np.random.randint(len(far))]
    return np.exp2(a.ravel()).repeat(32)


BF16 = ml_dtypes.bfloat16


def bf(x):
    return np.asarray(x, np.float32).astype(BF16)


def f64(x):
    return np.asarray(x).astype(np.float64)


B, C, T, P, N, D = 8, 16, 2048, 128, 8, 512
L = T // P
G = L // N


def draw0():
    s = mx_kscale(D)
    u = mx_kscale(P * N)
    un = u.reshape(P, N).T
    ut = np.tile(u, G)
    return {'h_enc': bf(np.random.standard_normal((N, B, C, G, D)) * 0.7 * s),
            'dec_W': bf(np.random.standard_normal((N, D, P)) / np.sqrt(D) / s[None, :, None] * un[:, None, :]),
            'dec_b': bf(np.random.standard_normal((N, P)) * 0.2 * un),
            'map_W': bf(np.random.standard_normal((T, T)) / np.sqrt(T) / ut[:, None]),
            'map_b': bf(np.random.standard_normal(T) * 0.2)}


def core(h_enc, dec_W, dec_b, map_W, map_b):
    h = f64(h_enc).reshape(N, B * C * G, D)
    r = (mxq(h, 2, 'e4m3') @ mxq(f64(dec_W), 1, 'e4m3')) + f64(dec_b)[:, None, :]
    r = r.reshape(N, B, C, G * P)
    x_rec = np.moveaxis(r, 0, -1).reshape(B * C, T)
    y_hat = (mxq(x_rec, 1, 'e4m3') @ mxq(f64(map_W), 0, 'e4m3')) + f64(map_b)
    return y_hat.reshape(B, C, T)


def e4m3fn_bytes(y):
    return np.clip(np.asarray(y, np.float64), -448.0, 448.0).astype(np.float32).astype(ml_dtypes.float8_e4m3fn).view(np.uint8)


def e4m3fn_values(b):
    return np.asarray(b, np.uint8).view(ml_dtypes.float8_e4m3fn).astype(np.float64)


def setup_inputs():
    d = draw0()
    x0 = np.asarray(d['map_W']).astype(np.float64)
    s = (np.max(np.abs(x0), axis=(1,), keepdims=True) / 448.0).astype(np.float32)
    out = {}
    for k, v in d.items():
        if k == 'map_W':
            out['map_W_bytes'] = e4m3fn_bytes(x0 / s.astype(np.float64))
            out['map_W_scale'] = s
        else:
            out[k] = v
    return out


def reference(h_enc, dec_W, dec_b, map_W_bytes, map_W_scale, map_b):
    return core(h_enc, dec_W, dec_b, e4m3fn_values(map_W_bytes) * map_W_scale.astype(np.float64), map_b)

@@ -1,0 +1,386 @@
+from contextlib import ExitStack
+
+import concourse.mybir as mybir
+from concourse.masks import make_identity
+
+F32 = mybir.dt.float32
+BF16 = mybir.dt.bfloat16
+U32 = mybir.dt.uint32
+U8 = mybir.dt.uint8
+FP8 = mybir.dt.float8_e4m3fn
+FP8X4 = mybir.dt.float8_e4m3fn_x4
+COPY = mybir.ActivationFunctionType.Copy
+MULT = mybir.AluOpType.mult
+ADD = mybir.AluOpType.add
+
+MODELS, SERIES, PATCHES, FEATURES, SAMPLES, TIME = 8, 128, 2, 512, 128, 2048
+FLOPS = 2 * MODELS * SERIES * PATCHES * FEATURES * SAMPLES + 2 * SERIES * TIME * TIME
+
+P = 128
+PASSES = 4
+CHUNK = 1024
+
+
+def tile_model_pb_kernel(tc, h_enc, dec_W, dec_b, map_W_bytes, map_W_scale, map_b, out):
+    nc = tc.nc
+    with ExitStack() as ctx:
+        keep = ctx.enter_context(tc.tile_pool(name="keep", bufs=1))
+        work = ctx.enter_context(tc.tile_pool(name="work", bufs=3))
+        psum = ctx.enter_context(tc.psum_pool(name="psum", bufs=4))
+        ctx.enter_context(tc.manual_schedule())
+
+        out2 = out.rearrange("b c s -> (b c) s")
+
+        scale_t = keep.tile([P, PASSES, 4], F32, name="scale_t")
+        nc.scalar.dma_start(out=scale_t[:], in_=map_W_scale.rearrange("(g p j) o -> p g (j o)", p=P, j=4))
+        scale = scale_t[:].rearrange("p g j -> p (g j)")
+
+        byte_tiles = {}
+
+        def load_bytes(half, g, lo, hi):
+            t = keep.tile([P, 4, hi - lo], U8, name="bytes_%d_%d_%d" % (half, g, lo), align_bytes=64)
+            c0 = half * CHUNK
+            nc.sync.dma_start(
+                out=t[:],
+                in_=map_W_bytes[512 * g : 512 * (g + 1), c0 + lo : c0 + hi].rearrange("(p j) s -> p j s", j=4),
+            )
+            byte_tiles.setdefault((half, g), []).append((lo, hi, t))
+
+        def bytes_of(half, g, j, lo, hi):
+            for a, b, t in byte_tiles[(half, g)]:
+                if a <= lo and hi <= b:
+                    return t[:, j, lo - a : hi - a].bitcast(FP8)
+            raise ValueError("columns are split over two loads")
+
+        dec_raw = []
+
+        def load_dec(i):
+            t = keep.tile([P, 4, 4, SAMPLES], BF16, name="dec_raw_%d" % i, align_bytes=64)
+            nc.sync.dma_start(out=t[:], in_=dec_W[4 * i : 4 * i + 4].rearrange("n (p j) w -> p n j w", j=4))
+            dec_raw.append(t)
+
+        h_raw = []
+
+        def load_h(i):
+            t = keep.tile([P, 2, PATCHES * FEATURES], BF16, name="h_raw_%d" % i, align_bytes=64)
+            nc.sync.dma_start(out=t[:], in_=h_enc[2 * i : 2 * i + 2].rearrange("n b c l d -> (b c) n (l d)"))
+            h_raw.append(t)
+
+        load_bytes(0, 0, 0, 512)
+        load_bytes(0, 0, 512, 1024)
+        load_dec(0)
+        load_bytes(0, 1, 0, 1024)
+        load_h(0)
+        load_dec(1)
+        load_h(1)
+        load_h(2)
+        load_h(3)
+        load_bytes(0, 2, 0, 1024)
+        decb_raw = keep.tile([P, MODELS, SAMPLES], BF16, name="decb_raw")
+        nc.sync.dma_start(
+            out=decb_raw[:].rearrange("p n q -> p (n q)"),
+            in_=dec_b.rearrange("n q -> (n q)").partition_broadcast(P),
+        )
+        load_bytes(0, 3, 0, 1024)
+        for g in range(PASSES):
+            load_bytes(1, g, 0, 1024)
+        mapb = keep.tile([P, TIME], BF16, name="mapb")
+        nc.sync.dma_start(out=mapb[:], in_=map_b.partition_broadcast(P))
+
+        ident = keep.tile([P, P], F32, name="ident")
+        make_identity(nc, ident[:])
+        warm = keep.tile([P, 1], F32, name="warm")
+        nc.vector.memset(warm[:], 0.0)
+        warm2 = keep.tile([P, 1], F32, name="warm2")
+        nc.scalar.activation(out=warm2[:], in_=warm[:], func=COPY)
+
+        planes = {}
+
+        def plane_tile(half, g):
+            if (half, g) not in planes:
+                pl = work.tile([P, 4, CHUNK], BF16, name="planes", bufs=4, align_bytes=64)
+                planes[(half, g)] = pl
+            return planes[(half, g)]
+
+        def widen_scalar(half, g, j, lo, hi):
+            nc.scalar.activation(
+                out=plane_tile(half, g)[:, j, lo:hi],
+                in_=bytes_of(half, g, j, lo, hi),
+                func=COPY,
+                scale=scale[:, 4 * g + j : 4 * g + j + 1],
+            )
+
+        def widen_vector(half, g, j, lo, hi):
+            nc.vector.tensor_scalar(
+                out=plane_tile(half, g)[:, j, lo:hi],
+                in0=bytes_of(half, g, j, lo, hi),
+                scalar1=scale[:, 4 * g + j : 4 * g + j + 1],
+                scalar2=None,
+                op0=MULT,
+            )
+
+        grouped = {}
+        codes = {}
+
+        def interleave(half, g, lo, hi):
+            gt = work.tile([P, 512, 4], BF16, name="grouped", bufs=4, align_bytes=64)
+            nc.vector.tensor_copy(
+                out=gt[:, 0 : hi - lo, :].rearrange("p (c i) j -> p c j i", i=4),
+                in_=plane_tile(half, g)[:, :, lo:hi].rearrange("p j (c i) -> p c j i", i=4),
+            )
+            grouped[(half, g, lo)] = gt
+
+        def quantize_map(half, g, lo, hi):
+            n = hi - lo
+            ct = keep.tile([P, n], U32, name="wc_%d_%d_%d" % (half, g, lo), align_bytes=64)
+            st = keep.tile([P, n], U8, name="ws_%d_%d_%d" % (half, g, lo), align_bytes=64)
+            nc.vector.quantize_mx(
+                out=ct[:].bitcast(FP8X4),
+                scales=st[:],
+                in_=grouped[(half, g, lo)][:, 0:n, :].rearrange("p s j -> p (s j)"),
+            )
+            codes[(half, g, lo)] = (ct, st)
+
+        dec_grp = []
+        dec_codes = []
+
+        def interleave_dec(i):
+            gt = keep.tile([P, 4, SAMPLES, 4], BF16, name="dec_grp_%d" % i, align_bytes=64)
+            nc.vector.tensor_copy(
+                out=gt[:].rearrange("p n (c i) j -> p n c j i", i=4),
+                in_=dec_raw[i][:].rearrange("p n j (c i) -> p n c j i", i=4),
+            )
+            dec_grp.append(gt)
+
+        def quantize_dec(i):
+            ct = keep.tile([P, 512], U32, name="dc_%d" % i, align_bytes=64)
+            st = keep.tile([P, 512], U8, name="ds_%d" % i, align_bytes=64)
+            nc.vector.quantize_mx(
+                out=ct[:].bitcast(FP8X4),
+                scales=st[:],
+                in_=dec_grp[i][:].rearrange("p n w j -> p (n w j)"),
+            )
+            dec_codes.append((ct, st))
+
+        h_bank = {}
+        h_grp = {}
+        h_codes = []
+
+        def transpose_h(n):
+            bank = psum.tile([P, PATCHES, 2, P], F32, name="tr")
+            words = h_raw[n // 2][:, n % 2, :].bitcast(F32)
+            for l in range(PATCHES):
+                for u in range(2):
+                    nc.tensor.transpose(bank[:, l, u, :], words[:, 256 * l + u : 256 * (l + 1) : 2], ident[:])
+            h_bank[n] = bank
+
+        def empty_h(n):
+            if n % 2 == 0:
+                h_grp[n // 2] = keep.tile([P, 2, PATCHES, P, 4], BF16, name="h_grp_%d" % (n // 2), align_bytes=64)
+            dst = h_grp[n // 2][:, n % 2, :, :, :].rearrange("p l r j -> p (l r j)").bitcast(F32)
+            nc.scalar.copy(
+                out=dst.rearrange("p (l r u) -> p l r u", l=PATCHES, u=2),
+                in_=h_bank[n][:].rearrange("p l u r -> p l r u"),
+            )
+
+        def quantize_h(i):
+            ct = keep.tile([P, 512], U32, name="hc_%d" % i, align_bytes=64)
+            st = keep.tile([P, 512], U8, name="hs_%d" % i, align_bytes=64)
+            nc.vector.quantize_mx(
+                out=ct[:].bitcast(FP8X4),
+                scales=st[:],
+                in_=h_grp[i][:].rearrange("p n l r j -> p (n l r j)"),
+            )
+            h_codes.append((ct, st))
+
+        r_bank = {}
+
+        def decode():
+            for g in range(PASSES):
+                bank = psum.tile([P, MODELS, 64], F32, name="acc")
+                r_bank[g] = bank
+            for n in range(MODELS):
+                hc, hs = h_codes[n // 2]
+                dc, ds = dec_codes[n // 4]
+                for g in range(PASSES):
+                    a = ((n % 2) * PATCHES + g // 2) * P
+                    b = (n % 4) * SAMPLES + (g % 2) * 64
+                    nc.tensor.matmul_mx(
+                        out=r_bank[g][:, n, :],
+                        lhsT=hc[:, a : a + P].bitcast(FP8X4),
+                        lhsT_scale=hs[:, a : a + P],
+                        rhs=dc[:, b : b + 64].bitcast(FP8X4),
+                        rhs_scale=ds[:, b : b + 64],
+                        start=True,
+                        stop=True,
+                    )
+
+        decb = keep.tile([P, SAMPLES, MODELS], BF16, name="decb")
+
+        def interleave_bias():
+            nc.vector.tensor_copy(
+                out=decb[:].rearrange("p (c i) n -> p c n i", i=4),
+                in_=decb_raw[:].rearrange("p n (c i) -> p c n i", i=4),
+            )
+
+        x_rows = {}
+        x_bank = {}
+        x_grp = {}
+        x_codes = {}
+
+        def empty_r(g):
+            xt = keep.tile([P, 64, MODELS], BF16, name="x_rows_%d" % g, align_bytes=64)
+            nc.vector.tensor_tensor(
+                out=xt[:],
+                in0=r_bank[g][:].rearrange("p n q -> p q n"),
+                in1=decb[:, 64 * (g % 2) : 64 * (g % 2) + 64, :],
+                op=ADD,
+            )
+            x_rows[g] = xt
+
+        def transpose_x(i):
+            bank = psum.tile([P, 2, 2, P], F32, name="tr")
+            for v in range(2):
+                words = x_rows[2 * i + v][:].rearrange("p q n -> p (q n)").bitcast(F32)
+                for u in range(2):
+                    nc.tensor.transpose(bank[:, v, u, :], words[:, u:256:2], ident[:])
+            x_bank[i] = bank
+
+        def empty_x(i):
+            xg = keep.tile([P, 2, P, 4], BF16, name="x_grp_%d" % i, align_bytes=64)
+            dst = xg[:].rearrange("p v r j -> p (v r j)").bitcast(F32)
+            nc.scalar.copy(
+                out=dst.rearrange("p (v r u) -> p v r u", v=2, u=2),
+                in_=x_bank[i][:].rearrange("p v u r -> p v r u"),
+            )
+            x_grp[i] = xg
+
+        def quantize_x(i):
+            ct = keep.tile([P, 256], U32, name="xc_%d" % i, align_bytes=64)
+            st = keep.tile([P, 256], U8, name="xs_%d" % i, align_bytes=64)
+            nc.vector.quantize_mx(
+                out=ct[:].bitcast(FP8X4),
+                scales=st[:],
+                in_=x_grp[i][:].rearrange("p v r j -> p (v r j)"),
+            )
+            x_codes[i] = (ct, st)
+
+        y_bank = {}
+
+        def multiply(half, g, lo, hi, width):
+            wc, ws = codes[(half, g, lo)] if (half, g, lo) in codes else codes[(half, g, lo - lo % 512)]
+            base = 0 if (half, g, lo) in codes else lo % 512
+            xc, xs = x_codes[g // 2]
+            a = (g % 2) * P
+            if g == 0:
+                bank = psum.tile([P, 512], F32, name="acc")
+                y_bank[(half, lo)] = bank
+            nc.tensor.matmul_mx(
+                out=y_bank[(half, lo)][:, 0:width],
+                lhsT=xc[:, a : a + P].bitcast(FP8X4),
+                lhsT_scale=xs[:, a : a + P],
+                rhs=wc[:, base : base + width].bitcast(FP8X4),
+                rhs_scale=ws[:, base : base + width],
+                start=(g == 0),
+                stop=(g == PASSES - 1),
+            )
+
+        def finish(half, lo, width):
+            c0 = half * CHUNK + lo
+            yt = work.tile([P, 512], F32, name="y_rows", bufs=4)
+            nc.vector.tensor_tensor(
+                out=yt[:, 0:width], in0=y_bank[(half, lo)][:, 0:width], in1=mapb[:, c0 : c0 + width], op=ADD
+            )
+            nc.sync.dma_start(out=out2[:, c0 : c0 + width], in_=yt[:, 0:width])
+
+        def widen_chunk(half, g):
+            for j in range(4):
+                widen_scalar(half, g, j, 0, 1024)
+
+        pending = []
+        x_ready = []
+        backlog = []
+
+        def multiply_unit(half, g, lo, hi):
+            cuts = [(lo, hi)]
+            if half == 1 and (lo, hi) == (512, 1024):
+                cuts = [(512, 768), (768, 1024)]
+            for a, b in cuts:
+                multiply(half, g, a, b, b - a)
+
+        def flush():
+            half, g, lo, hi = pending.pop()
+            quantize_map(half, g, lo, hi)
+            backlog.append((half, g, lo, hi))
+            if x_ready:
+                while backlog:
+                    multiply_unit(*backlog.pop(0))
+
+        def group(half, g, lo, hi):
+            interleave(half, g, lo, hi)
+            if pending:
+                flush()
+            pending.append((half, g, lo, hi))
+
+        for j in range(4):
+            widen_vector(0, 0, j, 0, 512)
+        for j in range(4):
+            widen_scalar(0, 0, j, 512, 1024)
+        group(0, 0, 0, 512)
+        interleave_dec(0)
+        flush()
+        group(0, 0, 512, 1024)
+        quantize_dec(0)
+        interleave_dec(1)
+        flush()
+        quantize_dec(1)
+
+        widen_chunk(0, 1)
+        for n in range(4):
+            transpose_h(n)
+        for n in range(4):
+            empty_h(n)
+        for n in range(4, 8):
+            transpose_h(n)
+        for n in range(4, 8):
+            empty_h(n)
+        group(0, 1, 0, 512)
+        group(0, 1, 512, 1024)
+        interleave_bias()
+        flush()
+        for i in range(4):
+            quantize_h(i)
+        widen_chunk(0, 2)
+        decode()
+        for g in range(PASSES):
+            empty_r(g)
+        for i in range(2):
+            transpose_x(i)
+        group(0, 2, 0, 512)
+        group(0, 2, 512, 1024)
+        widen_chunk(0, 3)
+        for i in range(2):
+            empty_x(i)
+        group(0, 3, 0, 512)
+        group(0, 3, 512, 1024)
+        for i in range(2):
+            quantize_x(i)
+        x_ready.append(True)
+
+        for g in range(PASSES - 1):
+            widen_chunk(1, g)
+            group(1, g, 0, 512)
+            group(1, g, 512, 1024)
+            if g == 0:
+                finish(0, 0, 512)
+                finish(0, 512, 512)
+
+        g = PASSES - 1
+        for lo, hi in ((0, 512), (512, 768), (768, 1024)):
+            for j in range(4):
+                widen_scalar(1, g, j, lo, hi)
+            group(1, g, lo, hi)
+        flush()
+        finish(1, 0, 512)
+        finish(1, 512, 256)
+        finish(1, 768, 256)

@@ -89,6 +89,8 @@ def tile_model_pb_kernel(tc, h_enc, dec_W, dec_b, map_W_bytes, map_W_scale, map_
 
         ident = keep.tile([P, P], F32, name="ident")
         make_identity(nc, ident[:])
+        ident16 = keep.tile([P, P], BF16, name="ident16")
+        make_identity(nc, ident16[:])
         warm = keep.tile([P, 1], F32, name="warm")
         nc.vector.memset(warm[:], 0.0)
         warm2 = keep.tile([P, 1], F32, name="warm2")
@@ -123,7 +125,7 @@ def tile_model_pb_kernel(tc, h_enc, dec_W, dec_b, map_W_bytes, map_W_scale, map_
         codes = {}
 
         def interleave(half, g, lo, hi):
-            gt = work.tile([P, 512, 4], BF16, name="grouped", bufs=4, align_bytes=64)
+            gt = work.tile([P, 1024, 4], BF16, name="grouped", bufs=3, align_bytes=64)
             nc.vector.tensor_copy(
                 out=gt[:, 0 : hi - lo, :].rearrange("p (c i) j -> p c j i", i=4),
                 in_=plane_tile(half, g)[:, :, lo:hi].rearrange("p j (c i) -> p c j i", i=4),
@@ -144,13 +146,35 @@ def tile_model_pb_kernel(tc, h_enc, dec_W, dec_b, map_W_bytes, map_W_scale, map_
         dec_grp = []
         dec_codes = []
 
-        def interleave_dec(i):
+        for i in range(2):
             gt = keep.tile([P, 4, SAMPLES, 4], BF16, name="dec_grp_%d" % i, align_bytes=64)
-            nc.vector.tensor_copy(
-                out=gt[:].rearrange("p n (c i) j -> p n c j i", i=4),
-                in_=dec_raw[i][:].rearrange("p n j (c i) -> p n c j i", i=4),
-            )
             dec_grp.append(gt)
+
+        def interleave_dec(i, lo, hi):
+            nc.vector.tensor_copy(
+                out=dec_grp[i][:, lo:hi, :, :].rearrange("p n (c i) j -> p n c j i", i=4),
+                in_=dec_raw[i][:, lo:hi, :, :].rearrange("p n j (c i) -> p n c j i", i=4),
+            )
+
+        dec_bank = {}
+
+        def shuffle_dec(i, k):
+            bank = psum.tile([P, 2, SAMPLES, 4], BF16, name="tr")
+            for v in range(2):
+                nc.tensor.matmul(
+                    out=bank[:, v, :, :],
+                    lhsT=ident16[:],
+                    rhs=dec_raw[i][:, 2 * k + v, :, :].rearrange("p j w -> p w j"),
+                    start=True,
+                    stop=True,
+                )
+            dec_bank[(i, k)] = bank
+
+        def empty_dec(i, k):
+            nc.scalar.copy(
+                out=dec_grp[i][:, 2 * k : 2 * k + 2, :, :].rearrange("p n w j -> p (n w j)"),
+                in_=dec_bank[(i, k)][:].rearrange("p n w j -> p (n w j)"),
+            )
 
         def quantize_dec(i):
             ct = keep.tile([P, 512], U32, name="dc_%d" % i, align_bytes=64)
@@ -267,20 +291,20 @@ def tile_model_pb_kernel(tc, h_enc, dec_W, dec_b, map_W_bytes, map_W_scale, map_
 
         y_bank = {}
 
-        def multiply(half, g, lo, hi, width):
-            wc, ws = codes[(half, g, lo)] if (half, g, lo) in codes else codes[(half, g, lo - lo % 512)]
-            base = 0 if (half, g, lo) in codes else lo % 512
+        def multiply(half, g, a, b, unit):
+            lo, hi = unit
+            wc, ws = codes[(half, g, lo)]
             xc, xs = x_codes[g // 2]
-            a = (g % 2) * P
+            m = (g % 2) * P
             if g == 0:
                 bank = psum.tile([P, 512], F32, name="acc")
-                y_bank[(half, lo)] = bank
+                y_bank[(half, a)] = bank
             nc.tensor.matmul_mx(
-                out=y_bank[(half, lo)][:, 0:width],
-                lhsT=xc[:, a : a + P].bitcast(FP8X4),
-                lhsT_scale=xs[:, a : a + P],
-                rhs=wc[:, base : base + width].bitcast(FP8X4),
-                rhs_scale=ws[:, base : base + width],
+                out=y_bank[(half, a)][:, 0 : b - a],
+                lhsT=xc[:, m : m + P].bitcast(FP8X4),
+                lhsT_scale=xs[:, m : m + P],
+                rhs=wc[:, a - lo : b - lo].bitcast(FP8X4),
+                rhs_scale=ws[:, a - lo : b - lo],
                 start=(g == 0),
                 stop=(g == PASSES - 1),
             )
@@ -293,20 +317,15 @@ def tile_model_pb_kernel(tc, h_enc, dec_W, dec_b, map_W_bytes, map_W_scale, map_
             )
             nc.sync.dma_start(out=out2[:, c0 : c0 + width], in_=yt[:, 0:width])
 
-        def widen_chunk(half, g):
-            for j in range(4):
-                widen_scalar(half, g, j, 0, 1024)
-
         pending = []
         x_ready = []
         backlog = []
 
         def multiply_unit(half, g, lo, hi):
-            cuts = [(lo, hi)]
-            if half == 1 and (lo, hi) == (512, 1024):
-                cuts = [(512, 768), (768, 1024)]
+            cuts = ((0, 512), (512, 1024)) if half == 0 else ((0, 512), (512, 768), (768, 1024))
             for a, b in cuts:
-                multiply(half, g, a, b, b - a)
+                if lo <= a and b <= hi:
+                    multiply(half, g, a, b, (lo, hi))
 
         def flush():
             half, g, lo, hi = pending.pop()
@@ -322,20 +341,49 @@ def tile_model_pb_kernel(tc, h_enc, dec_W, dec_b, map_W_bytes, map_W_scale, map_
                 flush()
             pending.append((half, g, lo, hi))
 
+        def widen(half, g, vector_planes):
+            for j in range(4):
+                if j not in vector_planes:
+                    widen_scalar(half, g, j, 0, 1024)
+            for j in vector_planes:
+                widen_vector(half, g, j, 0, 1024)
+
+        map_bank = {}
+
+        def shuffle_map(half, g, lo, hi):
+            bank = psum.tile([P, 256, 4], BF16, name="tr")
+            for b in range(lo, hi, 128):
+                nc.tensor.matmul(
+                    out=bank[:, b - lo : b - lo + 128, :],
+                    lhsT=ident16[:],
+                    rhs=planes[(half, g)][:, :, b : b + 128].rearrange("p j s -> p s j"),
+                    start=True,
+                    stop=True,
+                )
+            map_bank[(half, g, lo)] = bank
+
+        def empty_map(half, g, lo, hi):
+            gt = work.tile([P, 256, 4], BF16, name="grouped_pe", bufs=3, align_bytes=64)
+            nc.scalar.copy(
+                out=gt[:, 0 : hi - lo, :].rearrange("p s j -> p (s j)"),
+                in_=map_bank[(half, g, lo)][:].rearrange("p s j -> p (s j)"),
+            )
+            grouped[(half, g, lo)] = gt
+
         for j in range(4):
             widen_vector(0, 0, j, 0, 512)
         for j in range(4):
             widen_scalar(0, 0, j, 512, 1024)
         group(0, 0, 0, 512)
-        interleave_dec(0)
+        interleave_dec(0, 0, 4)
         flush()
+        widen(0, 1, ())
         group(0, 0, 512, 1024)
         quantize_dec(0)
-        interleave_dec(1)
+        interleave_dec(1, 0, 4)
         flush()
         quantize_dec(1)
 
-        widen_chunk(0, 1)
         for n in range(4):
             transpose_h(n)
         for n in range(4):
@@ -344,43 +392,48 @@ def tile_model_pb_kernel(tc, h_enc, dec_W, dec_b, map_W_bytes, map_W_scale, map_
             transpose_h(n)
         for n in range(4, 8):
             empty_h(n)
-        group(0, 1, 0, 512)
-        group(0, 1, 512, 1024)
+        group(0, 1, 0, 1024)
         interleave_bias()
         flush()
         for i in range(4):
             quantize_h(i)
-        widen_chunk(0, 2)
+        widen(0, 2, (3,))
         decode()
         for g in range(PASSES):
             empty_r(g)
         for i in range(2):
             transpose_x(i)
-        group(0, 2, 0, 512)
-        group(0, 2, 512, 1024)
-        widen_chunk(0, 3)
+        widen(0, 3, (3,))
+        group(0, 2, 0, 1024)
         for i in range(2):
             empty_x(i)
-        group(0, 3, 0, 512)
-        group(0, 3, 512, 1024)
+        group(0, 3, 0, 1024)
         for i in range(2):
             quantize_x(i)
         x_ready.append(True)
 
-        for g in range(PASSES - 1):
-            widen_chunk(1, g)
-            group(1, g, 0, 512)
-            group(1, g, 512, 1024)
-            if g == 0:
-                finish(0, 0, 512)
-                finish(0, 512, 512)
+        widen(1, 0, ())
+        group(1, 0, 0, 1024)
 
+        widen(1, 1, ())
+        group(1, 1, 0, 1024)
+        finish(0, 0, 512)
+        finish(0, 512, 512)
+        widen(1, 2, ())
+        group(1, 2, 0, 1024)
         g = PASSES - 1
-        for lo, hi in ((0, 512), (512, 768), (768, 1024)):
+        for lo, hi in ((0, 512), (512, 1024)):
             for j in range(4):
                 widen_scalar(1, g, j, lo, hi)
-            group(1, g, lo, hi)
+        shuffle_map(1, g, 512, 768)
+        shuffle_map(1, g, 768, 1024)
+        empty_map(1, g, 512, 768)
+        empty_map(1, g, 768, 1024)
+        group(1, g, 0, 512)
         flush()
+        for lo in (512, 768):
+            pending.append((1, g, lo, lo + 256))
+            flush()
         finish(1, 0, 512)
         finish(1, 512, 256)
         finish(1, 768, 256)

@@ -18,7 +18,8 @@ FLOPS = 2 * MODELS * SERIES * PATCHES * FEATURES * SAMPLES + 2 * SERIES * TIME *
 
 P = 128
 PASSES = 4
-CHUNK = 1024
+CUTS = ((0, 512), (512, 1024), (1024, 1536), (1536, 1792), (1792, 2048))
+PE_CUTS = (1536, 1792,)
 
 
 def tile_model_pb_kernel(tc, h_enc, dec_W, dec_b, map_W_bytes, map_W_scale, map_b, out):
@@ -26,30 +27,31 @@ def tile_model_pb_kernel(tc, h_enc, dec_W, dec_b, map_W_bytes, map_W_scale, map_
     with ExitStack() as ctx:
         keep = ctx.enter_context(tc.tile_pool(name="keep", bufs=1))
         work = ctx.enter_context(tc.tile_pool(name="work", bufs=3))
-        psum = ctx.enter_context(tc.psum_pool(name="psum", bufs=4))
+        psum = ctx.enter_context(tc.psum_pool(name="psum", bufs=3))
         ctx.enter_context(tc.manual_schedule())
 
         out2 = out.rearrange("b c s -> (b c) s")
 
-        scale_t = keep.tile([P, PASSES, 4], F32, name="scale_t")
-        nc.scalar.dma_start(out=scale_t[:], in_=map_W_scale.rearrange("(g p j) o -> p g (j o)", p=P, j=4))
-        scale = scale_t[:].rearrange("p g j -> p (g j)")
+        scale_view = map_W_scale.rearrange("(g p j) o -> g p (j o)", p=P, j=4)
+        scales_of = []
+
+        def load_scale(g, queue):
+            t = keep.tile([P, 4], F32, name="scale_%d" % g)
+            queue.dma_start(out=t[:], in_=scale_view[g])
+            scales_of.append(t)
 
         byte_tiles = {}
 
-        def load_bytes(half, g, lo, hi):
-            t = keep.tile([P, 4, hi - lo], U8, name="bytes_%d_%d_%d" % (half, g, lo), align_bytes=64)
-            c0 = half * CHUNK
-            nc.sync.dma_start(
-                out=t[:],
-                in_=map_W_bytes[512 * g : 512 * (g + 1), c0 + lo : c0 + hi].rearrange("(p j) s -> p j s", j=4),
-            )
-            byte_tiles.setdefault((half, g), []).append((lo, hi, t))
+        def load_bytes(g, lo, hi, j0=0, j1=4):
+            t = keep.tile([P, j1 - j0, hi - lo], U8, name="bytes_%d_%d_%d" % (g, lo, j0), align_bytes=64)
+            rows = map_W_bytes[512 * g : 512 * (g + 1), lo:hi].rearrange("(p j) s -> p j s", j=4)
+            nc.sync.dma_start(out=t[:], in_=rows[:, j0:j1, :])
+            byte_tiles.setdefault(g, []).append((lo, hi, j0, j1, t))
 
-        def bytes_of(half, g, j, lo, hi):
-            for a, b, t in byte_tiles[(half, g)]:
-                if a <= lo and hi <= b:
-                    return t[:, j, lo - a : hi - a].bitcast(FP8)
+        def bytes_of(g, j, lo, hi):
+            for a, b, j0, j1, t in byte_tiles[g]:
+                if a <= lo and hi <= b and j0 <= j < j1:
+                    return t[:, j - j0, lo - a : hi - a].bitcast(FP8)
             raise ValueError("columns are split over two loads")
 
         dec_raw = []
@@ -66,24 +68,31 @@ def tile_model_pb_kernel(tc, h_enc, dec_W, dec_b, map_W_bytes, map_W_scale, map_
             nc.sync.dma_start(out=t[:], in_=h_enc[2 * i : 2 * i + 2].rearrange("n b c l d -> (b c) n (l d)"))
             h_raw.append(t)
 
-        load_bytes(0, 0, 0, 512)
-        load_bytes(0, 0, 512, 1024)
+        decb_row = keep.tile([P, MODELS, SAMPLES], BF16, name="decb_row")
+        ones = keep.tile([P, P], BF16, name="ones")
+        nc.gpsimd.memset(decb_row[:], 0.0)
+        nc.gpsimd.memset(ones[:], 1.0)
+
+        def load_decb():
+            nc.sync.dma_start(out=decb_row[0:1, :, :], in_=dec_b.unsqueeze(0))
+
+        load_scale(0, nc.scalar)
+        for j in range(4):
+            load_bytes(0, 0, TIME, j, j + 1)
+        load_scale(1, nc.sync)
+        load_bytes(1, 0, TIME, 0, 2)
+        load_bytes(1, 0, TIME, 2, 4)
+        load_decb()
         load_dec(0)
-        load_bytes(0, 1, 0, 1024)
         load_h(0)
-        load_dec(1)
         load_h(1)
+        load_dec(1)
         load_h(2)
         load_h(3)
-        load_bytes(0, 2, 0, 1024)
-        decb_raw = keep.tile([P, MODELS, SAMPLES], BF16, name="decb_raw")
-        nc.sync.dma_start(
-            out=decb_raw[:].rearrange("p n q -> p (n q)"),
-            in_=dec_b.rearrange("n q -> (n q)").partition_broadcast(P),
-        )
-        load_bytes(0, 3, 0, 1024)
-        for g in range(PASSES):
-            load_bytes(1, g, 0, 1024)
+        for g in range(2, PASSES):
+            load_scale(g, nc.sync)
+            load_bytes(g, 0, TIME, 0, 2)
+            load_bytes(g, 0, TIME, 2, 4)
         mapb = keep.tile([P, TIME], BF16, name="mapb")
         nc.sync.dma_start(out=mapb[:], in_=map_b.partition_broadcast(P))
 
@@ -98,83 +107,132 @@ def tile_model_pb_kernel(tc, h_enc, dec_W, dec_b, map_W_bytes, map_W_scale, map_
 
         planes = {}
 
-        def plane_tile(half, g):
-            if (half, g) not in planes:
-                pl = work.tile([P, 4, CHUNK], BF16, name="planes", bufs=4, align_bytes=64)
-                planes[(half, g)] = pl
-            return planes[(half, g)]
+        def plane_of(g, j, lo, hi):
+            half = lo // 1024
+            if (g, half) not in planes:
+                pl = work.tile([P, 4, 1024], BF16, name="planes", bufs=4, align_bytes=64)
+                planes[(g, half)] = pl
+            return planes[(g, half)][:, j, lo - 1024 * half : hi - 1024 * half]
 
-        def widen_scalar(half, g, j, lo, hi):
+        def widen_scalar(g, j, lo, hi):
             nc.scalar.activation(
-                out=plane_tile(half, g)[:, j, lo:hi],
-                in_=bytes_of(half, g, j, lo, hi),
-                func=COPY,
-                scale=scale[:, 4 * g + j : 4 * g + j + 1],
+                out=plane_of(g, j, lo, hi), in_=bytes_of(g, j, lo, hi), func=COPY, scale=scales_of[g][:, j : j + 1]
             )
 
-        def widen_vector(half, g, j, lo, hi):
+        def widen_vector(g, j, lo, hi):
             nc.vector.tensor_scalar(
-                out=plane_tile(half, g)[:, j, lo:hi],
-                in0=bytes_of(half, g, j, lo, hi),
-                scalar1=scale[:, 4 * g + j : 4 * g + j + 1],
+                out=plane_of(g, j, lo, hi),
+                in0=bytes_of(g, j, lo, hi),
+                scalar1=scales_of[g][:, j : j + 1],
                 scalar2=None,
                 op0=MULT,
             )
 
         grouped = {}
         codes = {}
+        pending = []
+        x_ready = []
+        backlog = []
+        y_bank = {}
+        x_codes = {}
 
-        def interleave(half, g, lo, hi):
+        def interleave(g, lo, hi):
+            half = lo // 1024
+            a, b = lo - 1024 * half, hi - 1024 * half
             gt = work.tile([P, 1024, 4], BF16, name="grouped", bufs=3, align_bytes=64)
             nc.vector.tensor_copy(
                 out=gt[:, 0 : hi - lo, :].rearrange("p (c i) j -> p c j i", i=4),
-                in_=plane_tile(half, g)[:, :, lo:hi].rearrange("p j (c i) -> p c j i", i=4),
+                in_=planes[(g, half)][:, :, a:b].rearrange("p j (c i) -> p c j i", i=4),
             )
-            grouped[(half, g, lo)] = gt
+            grouped[(g, lo)] = gt
 
-        def quantize_map(half, g, lo, hi):
-            n = hi - lo
-            ct = keep.tile([P, n], U32, name="wc_%d_%d_%d" % (half, g, lo), align_bytes=64)
-            st = keep.tile([P, n], U8, name="ws_%d_%d_%d" % (half, g, lo), align_bytes=64)
-            nc.vector.quantize_mx(
-                out=ct[:].bitcast(FP8X4),
-                scales=st[:],
-                in_=grouped[(half, g, lo)][:, 0:n, :].rearrange("p s j -> p (s j)"),
-            )
-            codes[(half, g, lo)] = (ct, st)
+        map_bank = {}
 
-        dec_grp = []
-        dec_codes = []
-
-        for i in range(2):
-            gt = keep.tile([P, 4, SAMPLES, 4], BF16, name="dec_grp_%d" % i, align_bytes=64)
-            dec_grp.append(gt)
-
-        def interleave_dec(i, lo, hi):
-            nc.vector.tensor_copy(
-                out=dec_grp[i][:, lo:hi, :, :].rearrange("p n (c i) j -> p n c j i", i=4),
-                in_=dec_raw[i][:, lo:hi, :, :].rearrange("p n j (c i) -> p n c j i", i=4),
-            )
-
-        dec_bank = {}
-
-        def shuffle_dec(i, k):
-            bank = psum.tile([P, 2, SAMPLES, 4], BF16, name="tr")
-            for v in range(2):
+        def shuffle_map(g, lo, hi):
+            pl = planes[(g, lo // 1024)]
+            a = lo % 1024
+            bank = psum.tile([P, 256, 4], BF16, name="tr")
+            for b in (0, 128):
                 nc.tensor.matmul(
-                    out=bank[:, v, :, :],
+                    out=bank[:, b : b + 128, :],
                     lhsT=ident16[:],
-                    rhs=dec_raw[i][:, 2 * k + v, :, :].rearrange("p j w -> p w j"),
+                    rhs=pl[:, :, a + b : a + b + 128].rearrange("p j s -> p s j"),
                     start=True,
                     stop=True,
                 )
-            dec_bank[(i, k)] = bank
+            map_bank[(g, lo)] = bank
 
-        def empty_dec(i, k):
+        def empty_map(g, lo):
+            gt = work.tile([P, 256, 4], BF16, name="grouped_pe", bufs=3, align_bytes=64)
             nc.scalar.copy(
-                out=dec_grp[i][:, 2 * k : 2 * k + 2, :, :].rearrange("p n w j -> p (n w j)"),
-                in_=dec_bank[(i, k)][:].rearrange("p n w j -> p (n w j)"),
+                out=gt[:].rearrange("p s j -> p (s j)"), in_=map_bank[(g, lo)][:].rearrange("p s j -> p (s j)")
             )
+            grouped[(g, lo)] = gt
+
+        def multiply(g, lo, hi):
+            wc, ws = codes[(g, lo)]
+            xc, xs = x_codes[g // 2]
+            m = (g % 2) * P
+            for a, b in CUTS:
+                c, d = max(a, lo), min(b, hi)
+                if c < d:
+                    if g == 0:
+                        bank = psum.tile([P, 512], F32, name="acc", bufs=5)
+                        y_bank[a] = bank
+                    nc.tensor.matmul_mx(
+                        out=y_bank[a][:, c - a : d - a],
+                        lhsT=xc[:, m : m + P].bitcast(FP8X4),
+                        lhsT_scale=xs[:, m : m + P],
+                        rhs=wc[:, c - lo : d - lo].bitcast(FP8X4),
+                        rhs_scale=ws[:, c - lo : d - lo],
+                        start=(g == 0),
+                        stop=(g == (2 if c in PE_CUTS or (c == 1024 and d == 1280) else 3)),
+                    )
+
+        def flush():
+            g, lo, hi = pending.pop()
+            n = hi - lo
+            ct = keep.tile([P, n], U32, name="wc_%d_%d" % (g, lo), align_bytes=64)
+            st = keep.tile([P, n], U8, name="ws_%d_%d" % (g, lo), align_bytes=64)
+            nc.vector.quantize_mx(
+                out=ct[:].bitcast(FP8X4),
+                scales=st[:],
+                in_=grouped[(g, lo)][:, 0:n, :].rearrange("p s j -> p (s j)"),
+            )
+            codes[(g, lo)] = (ct, st)
+            backlog.append((g, lo, hi))
+            if x_ready:
+                while backlog:
+                    multiply(*backlog.pop(0))
+
+        def group(g, lo, hi):
+            interleave(g, lo, hi)
+            if pending:
+                flush()
+            pending.append((g, lo, hi))
+
+        def finish(a, b):
+            yt = work.tile([P, 512], F32, name="y_rows", bufs=5)
+            nc.vector.tensor_tensor(out=yt[:, 0 : b - a], in0=y_bank[a][:, 0 : b - a], in1=mapb[:, a:b], op=ADD)
+            nc.sync.dma_start(out=out2[:, a:b], in_=yt[:, 0 : b - a])
+
+        def widen(g, lo, hi, vector_planes=()):
+            for j in range(4):
+                if j not in vector_planes:
+                    widen_scalar(g, j, lo, hi)
+            for j in vector_planes:
+                widen_vector(g, j, lo, hi)
+
+        dec_grp = {}
+        dec_codes = []
+
+        def interleave_dec(i):
+            gt = keep.tile([P, 4, SAMPLES, 4], BF16, name="dec_grp_%d" % i, align_bytes=64)
+            nc.vector.tensor_copy(
+                out=gt[:].rearrange("p n (c i) j -> p n c j i", i=4),
+                in_=dec_raw[i][:].rearrange("p n j (c i) -> p n c j i", i=4),
+            )
+            dec_grp[i] = gt
 
         def quantize_dec(i):
             ct = keep.tile([P, 512], U32, name="dc_%d" % i, align_bytes=64)
@@ -185,6 +243,26 @@ def tile_model_pb_kernel(tc, h_enc, dec_W, dec_b, map_W_bytes, map_W_scale, map_
                 in_=dec_grp[i][:].rearrange("p n w j -> p (n w j)"),
             )
             dec_codes.append((ct, st))
+
+        decb = keep.tile([P, SAMPLES, MODELS], BF16, name="decb")
+        decb_bank = []
+
+        def spread_bias():
+            bank = psum.tile([P, SAMPLES, MODELS], BF16, name="tr")
+            for q in (0, 64):
+                nc.tensor.matmul(
+                    out=bank[:, q : q + 64, :],
+                    lhsT=ones[:],
+                    rhs=decb_row[:, :, q : q + 64].rearrange("p n q -> p q n"),
+                    start=True,
+                    stop=True,
+                )
+            decb_bank.append(bank)
+
+        def empty_bias():
+            nc.scalar.copy(
+                out=decb[:].rearrange("p q n -> p (q n)"), in_=decb_bank[0][:].rearrange("p q n -> p (q n)")
+            )
 
         h_bank = {}
         h_grp = {}
@@ -200,7 +278,8 @@ def tile_model_pb_kernel(tc, h_enc, dec_W, dec_b, map_W_bytes, map_W_scale, map_
 
         def empty_h(n):
             if n % 2 == 0:
-                h_grp[n // 2] = keep.tile([P, 2, PATCHES, P, 4], BF16, name="h_grp_%d" % (n // 2), align_bytes=64)
+                gt = keep.tile([P, 2, PATCHES, P, 4], BF16, name="h_grp_%d" % (n // 2), align_bytes=64)
+                h_grp[n // 2] = gt
             dst = h_grp[n // 2][:, n % 2, :, :, :].rearrange("p l r j -> p (l r j)").bitcast(F32)
             nc.scalar.copy(
                 out=dst.rearrange("p (l r u) -> p l r u", l=PATCHES, u=2),
@@ -219,38 +298,28 @@ def tile_model_pb_kernel(tc, h_enc, dec_W, dec_b, map_W_bytes, map_W_scale, map_
 
         r_bank = {}
 
-        def decode():
+        def decode(n):
+            hc, hs = h_codes[n // 2]
+            dc, ds = dec_codes[n // 4]
             for g in range(PASSES):
-                bank = psum.tile([P, MODELS, 64], F32, name="acc")
-                r_bank[g] = bank
-            for n in range(MODELS):
-                hc, hs = h_codes[n // 2]
-                dc, ds = dec_codes[n // 4]
-                for g in range(PASSES):
-                    a = ((n % 2) * PATCHES + g // 2) * P
-                    b = (n % 4) * SAMPLES + (g % 2) * 64
-                    nc.tensor.matmul_mx(
-                        out=r_bank[g][:, n, :],
-                        lhsT=hc[:, a : a + P].bitcast(FP8X4),
-                        lhsT_scale=hs[:, a : a + P],
-                        rhs=dc[:, b : b + 64].bitcast(FP8X4),
-                        rhs_scale=ds[:, b : b + 64],
-                        start=True,
-                        stop=True,
-                    )
-
-        decb = keep.tile([P, SAMPLES, MODELS], BF16, name="decb")
-
-        def interleave_bias():
-            nc.vector.tensor_copy(
-                out=decb[:].rearrange("p (c i) n -> p c n i", i=4),
-                in_=decb_raw[:].rearrange("p n (c i) -> p c n i", i=4),
-            )
+                if n == 0:
+                    bank = psum.tile([P, MODELS, 64], F32, name="acc", bufs=5)
+                    r_bank[g] = bank
+                a = ((n % 2) * PATCHES + g // 2) * P
+                b = (n % 4) * SAMPLES + (g % 2) * 64
+                nc.tensor.matmul_mx(
+                    out=r_bank[g][:, n, :],
+                    lhsT=hc[:, a : a + P].bitcast(FP8X4),
+                    lhsT_scale=hs[:, a : a + P],
+                    rhs=dc[:, b : b + 64].bitcast(FP8X4),
+                    rhs_scale=ds[:, b : b + 64],
+                    start=True,
+                    stop=True,
+                )
 
         x_rows = {}
         x_bank = {}
         x_grp = {}
-        x_codes = {}
 
         def empty_r(g):
             xt = keep.tile([P, 64, MODELS], BF16, name="x_rows_%d" % g, align_bytes=64)
@@ -289,151 +358,70 @@ def tile_model_pb_kernel(tc, h_enc, dec_W, dec_b, map_W_bytes, map_W_scale, map_
             )
             x_codes[i] = (ct, st)
 
-        y_bank = {}
-
-        def multiply(half, g, a, b, unit):
-            lo, hi = unit
-            wc, ws = codes[(half, g, lo)]
-            xc, xs = x_codes[g // 2]
-            m = (g % 2) * P
-            if g == 0:
-                bank = psum.tile([P, 512], F32, name="acc")
-                y_bank[(half, a)] = bank
-            nc.tensor.matmul_mx(
-                out=y_bank[(half, a)][:, 0 : b - a],
-                lhsT=xc[:, m : m + P].bitcast(FP8X4),
-                lhsT_scale=xs[:, m : m + P],
-                rhs=wc[:, a - lo : b - lo].bitcast(FP8X4),
-                rhs_scale=ws[:, a - lo : b - lo],
-                start=(g == 0),
-                stop=(g == PASSES - 1),
-            )
-
-        def finish(half, lo, width):
-            c0 = half * CHUNK + lo
-            yt = work.tile([P, 512], F32, name="y_rows", bufs=4)
-            nc.vector.tensor_tensor(
-                out=yt[:, 0:width], in0=y_bank[(half, lo)][:, 0:width], in1=mapb[:, c0 : c0 + width], op=ADD
-            )
-            nc.sync.dma_start(out=out2[:, c0 : c0 + width], in_=yt[:, 0:width])
-
-        pending = []
-        x_ready = []
-        backlog = []
-
-        def multiply_unit(half, g, lo, hi):
-            cuts = ((0, 512), (512, 1024)) if half == 0 else ((0, 512), (512, 768), (768, 1024))
-            for a, b in cuts:
-                if lo <= a and b <= hi:
-                    multiply(half, g, a, b, (lo, hi))
-
-        def flush():
-            half, g, lo, hi = pending.pop()
-            quantize_map(half, g, lo, hi)
-            backlog.append((half, g, lo, hi))
-            if x_ready:
-                while backlog:
-                    multiply_unit(*backlog.pop(0))
-
-        def group(half, g, lo, hi):
-            interleave(half, g, lo, hi)
-            if pending:
-                flush()
-            pending.append((half, g, lo, hi))
-
-        def widen(half, g, vector_planes):
-            for j in range(4):
-                if j not in vector_planes:
-                    widen_scalar(half, g, j, 0, 1024)
-            for j in vector_planes:
-                widen_vector(half, g, j, 0, 1024)
-
-        map_bank = {}
-
-        def shuffle_map(half, g, lo, hi):
-            bank = psum.tile([P, 256, 4], BF16, name="tr")
-            for b in range(lo, hi, 128):
-                nc.tensor.matmul(
-                    out=bank[:, b - lo : b - lo + 128, :],
-                    lhsT=ident16[:],
-                    rhs=planes[(half, g)][:, :, b : b + 128].rearrange("p j s -> p s j"),
-                    start=True,
-                    stop=True,
-                )
-            map_bank[(half, g, lo)] = bank
-
-        def empty_map(half, g, lo, hi):
-            gt = work.tile([P, 256, 4], BF16, name="grouped_pe", bufs=3, align_bytes=64)
-            nc.scalar.copy(
-                out=gt[:, 0 : hi - lo, :].rearrange("p s j -> p (s j)"),
-                in_=map_bank[(half, g, lo)][:].rearrange("p s j -> p (s j)"),
-            )
-            grouped[(half, g, lo)] = gt
-
-        for j in range(4):
-            widen_vector(0, 0, j, 0, 512)
-        for j in range(4):
-            widen_scalar(0, 0, j, 512, 1024)
-        group(0, 0, 0, 512)
-        interleave_dec(0, 0, 4)
+        for lo, j in ((0, 1), (1024, 1), (1024, 2), (1024, 3)):
+            widen_scalar(0, j, lo, lo + 1024)
+        for lo, j in ((0, 0), (1024, 0), (0, 2), (0, 3)):
+            widen_vector(0, j, lo, lo + 1024)
+        group(0, 0, 1024)
+        widen(1, 0, 1024)
+        group(0, 1024, 2048)
         flush()
-        widen(0, 1, ())
-        group(0, 0, 512, 1024)
-        quantize_dec(0)
-        interleave_dec(1, 0, 4)
-        flush()
-        quantize_dec(1)
-
-        for n in range(4):
+        for i in range(2):
+            interleave_dec(i)
+        for i in range(2):
+            quantize_dec(i)
+        spread_bias()
+        for n in range(MODELS):
             transpose_h(n)
-        for n in range(4):
+            if n % 2 == 0 and n // 2 not in (2, 3):
+                widen_scalar(1, n // 2, 1024, 2048)
+            if n == 1:
+                empty_bias()
             empty_h(n)
-        for n in range(4, 8):
-            transpose_h(n)
-        for n in range(4, 8):
-            empty_h(n)
-        group(0, 1, 0, 1024)
-        interleave_bias()
-        flush()
+        for j in (2, 3):
+            widen_vector(1, j, 1024, 2048)
+        group(1, 0, 1024)
+        group(1, 1024, 2048)
         for i in range(4):
             quantize_h(i)
-        widen(0, 2, (3,))
-        decode()
+        for n in range(MODELS):
+            decode(n)
+        widen(2, 0, 1024)
+        flush()
+        group(2, 0, 1024)
         for g in range(PASSES):
             empty_r(g)
+
         for i in range(2):
             transpose_x(i)
-        widen(0, 3, (3,))
-        group(0, 2, 0, 1024)
-        for i in range(2):
-            empty_x(i)
-        group(0, 3, 0, 1024)
+        widen(2, 1024, 2048)
+        for lo in PE_CUTS:
+            shuffle_map(2, lo, lo + 256)
+        for j in range(4):
+            widen_scalar(3, j, 0, 1024)
+            if j in (1, 2):
+                empty_x(j - 1)
+        flush()
+        group(2, 1024, 1536)
         for i in range(2):
             quantize_x(i)
         x_ready.append(True)
 
-        widen(1, 0, ())
-        group(1, 0, 0, 1024)
+        group(3, 0, 1024)
 
-        widen(1, 1, ())
-        group(1, 1, 0, 1024)
-        finish(0, 0, 512)
-        finish(0, 512, 512)
-        widen(1, 2, ())
-        group(1, 2, 0, 1024)
-        g = PASSES - 1
-        for lo, hi in ((0, 512), (512, 1024)):
-            for j in range(4):
-                widen_scalar(1, g, j, lo, hi)
-        shuffle_map(1, g, 512, 768)
-        shuffle_map(1, g, 768, 1024)
-        empty_map(1, g, 512, 768)
-        empty_map(1, g, 768, 1024)
-        group(1, g, 0, 512)
+        widen(3, 1024, 1536)
+        group(3, 1024, 1536)
+        widen(3, 1536, 1792)
+        empty_map(2, PE_CUTS[0])
+        group(3, 1536, 1792)
+        widen(3, 1792, 2048)
+        empty_map(2, PE_CUTS[1])
+        group(3, 1792, 2048)
+        finish(0, 512)
+        finish(512, 1024)
         flush()
-        for lo in (512, 768):
-            pending.append((1, g, lo, lo + 256))
+        for lo in PE_CUTS:
+            pending.append((2, lo, lo + 256))
             flush()
-        finish(1, 0, 512)
-        finish(1, 512, 256)
-        finish(1, 768, 256)
+        for a, b in CUTS[2:]:
+            finish(a, b)

from contextlib import ExitStack

import concourse.mybir as mybir
from concourse.masks import make_identity

F32 = mybir.dt.float32
BF16 = mybir.dt.bfloat16
U32 = mybir.dt.uint32
U8 = mybir.dt.uint8
FP8 = mybir.dt.float8_e4m3fn
FP8X4 = mybir.dt.float8_e4m3fn_x4
COPY = mybir.ActivationFunctionType.Copy
MULT = mybir.AluOpType.mult
ADD = mybir.AluOpType.add

MODELS, SERIES, PATCHES, FEATURES, SAMPLES, TIME = 8, 128, 2, 512, 128, 2048
FLOPS = 2 * MODELS * SERIES * PATCHES * FEATURES * SAMPLES + 2 * SERIES * TIME * TIME

P = 128
PASSES = 4
CUTS = ((0, 512), (512, 1024), (1024, 1536), (1536, 1792), (1792, 2048))
PE_CUTS = (1536, 1792,)


def tile_model_pb_kernel(tc, h_enc, dec_W, dec_b, map_W_bytes, map_W_scale, map_b, out):
    nc = tc.nc
    with ExitStack() as ctx:
        keep = ctx.enter_context(tc.tile_pool(name="keep", bufs=1))
        work = ctx.enter_context(tc.tile_pool(name="work", bufs=3))
        psum = ctx.enter_context(tc.psum_pool(name="psum", bufs=3))
        ctx.enter_context(tc.manual_schedule())

        out2 = out.rearrange("b c s -> (b c) s")

        scale_view = map_W_scale.rearrange("(g p j) o -> g p (j o)", p=P, j=4)
        scales_of = []

        def load_scale(g, queue):
            t = keep.tile([P, 4], F32, name="scale_%d" % g)
            queue.dma_start(out=t[:], in_=scale_view[g])
            scales_of.append(t)

        byte_tiles = {}

        def load_bytes(g, lo, hi, j0=0, j1=4):
            t = keep.tile([P, j1 - j0, hi - lo], U8, name="bytes_%d_%d_%d" % (g, lo, j0), align_bytes=64)
            rows = map_W_bytes[512 * g : 512 * (g + 1), lo:hi].rearrange("(p j) s -> p j s", j=4)
            nc.sync.dma_start(out=t[:], in_=rows[:, j0:j1, :])
            byte_tiles.setdefault(g, []).append((lo, hi, j0, j1, t))

        def bytes_of(g, j, lo, hi):
            for a, b, j0, j1, t in byte_tiles[g]:
                if a <= lo and hi <= b and j0 <= j < j1:
                    return t[:, j - j0, lo - a : hi - a].bitcast(FP8)
            raise ValueError("columns are split over two loads")

        dec_raw = []

        def load_dec(i):
            t = keep.tile([P, 4, 4, SAMPLES], BF16, name="dec_raw_%d" % i, align_bytes=64)
            nc.sync.dma_start(out=t[:], in_=dec_W[4 * i : 4 * i + 4].rearrange("n (p j) w -> p n j w", j=4))
            dec_raw.append(t)

        h_raw = []

        def load_h(i):
            t = keep.tile([P, 2, PATCHES * FEATURES], BF16, name="h_raw_%d" % i, align_bytes=64)
            nc.sync.dma_start(out=t[:], in_=h_enc[2 * i : 2 * i + 2].rearrange("n b c l d -> (b c) n (l d)"))
            h_raw.append(t)

        decb_row = keep.tile([P, MODELS, SAMPLES], BF16, name="decb_row")
        ones = keep.tile([P, P], BF16, name="ones")
        nc.gpsimd.memset(decb_row[:], 0.0)
        nc.gpsimd.memset(ones[:], 1.0)

        def load_decb():
            nc.sync.dma_start(out=decb_row[0:1, :, :], in_=dec_b.unsqueeze(0))

        load_scale(0, nc.scalar)
        for j in range(4):
            load_bytes(0, 0, TIME, j, j + 1)
        load_scale(1, nc.sync)
        load_bytes(1, 0, TIME, 0, 2)
        load_bytes(1, 0, TIME, 2, 4)
        load_decb()
        load_dec(0)
        load_h(0)
        load_h(1)
        load_dec(1)
        load_h(2)
        load_h(3)
        for g in range(2, PASSES):
            load_scale(g, nc.sync)
            load_bytes(g, 0, TIME, 0, 2)
            load_bytes(g, 0, TIME, 2, 4)
        mapb = keep.tile([P, TIME], BF16, name="mapb")
        nc.sync.dma_start(out=mapb[:], in_=map_b.partition_broadcast(P))

        ident = keep.tile([P, P], F32, name="ident")
        make_identity(nc, ident[:])
        ident16 = keep.tile([P, P], BF16, name="ident16")
        make_identity(nc, ident16[:])
        warm = keep.tile([P, 1], F32, name="warm")
        nc.vector.memset(warm[:], 0.0)
        warm2 = keep.tile([P, 1], F32, name="warm2")
        nc.scalar.activation(out=warm2[:], in_=warm[:], func=COPY)

        planes = {}

        def plane_of(g, j, lo, hi):
            half = lo // 1024
            if (g, half) not in planes:
                pl = work.tile([P, 4, 1024], BF16, name="planes", bufs=4, align_bytes=64)
                planes[(g, half)] = pl
            return planes[(g, half)][:, j, lo - 1024 * half : hi - 1024 * half]

        def widen_scalar(g, j, lo, hi):
            nc.scalar.activation(
                out=plane_of(g, j, lo, hi), in_=bytes_of(g, j, lo, hi), func=COPY, scale=scales_of[g][:, j : j + 1]
            )

        def widen_vector(g, j, lo, hi):
            nc.vector.tensor_scalar(
                out=plane_of(g, j, lo, hi),
                in0=bytes_of(g, j, lo, hi),
                scalar1=scales_of[g][:, j : j + 1],
                scalar2=None,
                op0=MULT,
            )

        grouped = {}
        codes = {}
        pending = []
        x_ready = []
        backlog = []
        y_bank = {}
        x_codes = {}

        def interleave(g, lo, hi):
            half = lo // 1024
            a, b = lo - 1024 * half, hi - 1024 * half
            gt = work.tile([P, 1024, 4], BF16, name="grouped", bufs=3, align_bytes=64)
            nc.vector.tensor_copy(
                out=gt[:, 0 : hi - lo, :].rearrange("p (c i) j -> p c j i", i=4),
                in_=planes[(g, half)][:, :, a:b].rearrange("p j (c i) -> p c j i", i=4),
            )
            grouped[(g, lo)] = gt

        map_bank = {}

        def shuffle_map(g, lo, hi):
            pl = planes[(g, lo // 1024)]
            a = lo % 1024
            bank = psum.tile([P, 256, 4], BF16, name="tr")
            for b in (0, 128):
                nc.tensor.matmul(
                    out=bank[:, b : b + 128, :],
                    lhsT=ident16[:],
                    rhs=pl[:, :, a + b : a + b + 128].rearrange("p j s -> p s j"),
                    start=True,
                    stop=True,
                )
            map_bank[(g, lo)] = bank

        def empty_map(g, lo):
            gt = work.tile([P, 256, 4], BF16, name="grouped_pe", bufs=3, align_bytes=64)
            nc.scalar.copy(
                out=gt[:].rearrange("p s j -> p (s j)"), in_=map_bank[(g, lo)][:].rearrange("p s j -> p (s j)")
            )
            grouped[(g, lo)] = gt

        def multiply(g, lo, hi):
            wc, ws = codes[(g, lo)]
            xc, xs = x_codes[g // 2]
            m = (g % 2) * P
            for a, b in CUTS:
                c, d = max(a, lo), min(b, hi)
                if c < d:
                    if g == 0:
                        bank = psum.tile([P, 512], F32, name="acc", bufs=5)
                        y_bank[a] = bank
                    nc.tensor.matmul_mx(
                        out=y_bank[a][:, c - a : d - a],
                        lhsT=xc[:, m : m + P].bitcast(FP8X4),
                        lhsT_scale=xs[:, m : m + P],
                        rhs=wc[:, c - lo : d - lo].bitcast(FP8X4),
                        rhs_scale=ws[:, c - lo : d - lo],
                        start=(g == 0),
                        stop=(g == (2 if c in PE_CUTS or (c == 1024 and d == 1280) else 3)),
                    )

        def flush():
            g, lo, hi = pending.pop()
            n = hi - lo
            ct = keep.tile([P, n], U32, name="wc_%d_%d" % (g, lo), align_bytes=64)
            st = keep.tile([P, n], U8, name="ws_%d_%d" % (g, lo), align_bytes=64)
            nc.vector.quantize_mx(
                out=ct[:].bitcast(FP8X4),
                scales=st[:],
                in_=grouped[(g, lo)][:, 0:n, :].rearrange("p s j -> p (s j)"),
            )
            codes[(g, lo)] = (ct, st)
            backlog.append((g, lo, hi))
            if x_ready:
                while backlog:
                    multiply(*backlog.pop(0))

        def group(g, lo, hi):
            interleave(g, lo, hi)
            if pending:
                flush()
            pending.append((g, lo, hi))

        def finish(a, b):
            yt = work.tile([P, 512], F32, name="y_rows", bufs=5)
            nc.vector.tensor_tensor(out=yt[:, 0 : b - a], in0=y_bank[a][:, 0 : b - a], in1=mapb[:, a:b], op=ADD)
            nc.sync.dma_start(out=out2[:, a:b], in_=yt[:, 0 : b - a])

        def widen(g, lo, hi, vector_planes=()):
            for j in range(4):
                if j not in vector_planes:
                    widen_scalar(g, j, lo, hi)
            for j in vector_planes:
                widen_vector(g, j, lo, hi)

        dec_grp = {}
        dec_codes = []

        def interleave_dec(i):
            gt = keep.tile([P, 4, SAMPLES, 4], BF16, name="dec_grp_%d" % i, align_bytes=64)
            nc.vector.tensor_copy(
                out=gt[:].rearrange("p n (c i) j -> p n c j i", i=4),
                in_=dec_raw[i][:].rearrange("p n j (c i) -> p n c j i", i=4),
            )
            dec_grp[i] = gt

        def quantize_dec(i):
            ct = keep.tile([P, 512], U32, name="dc_%d" % i, align_bytes=64)
            st = keep.tile([P, 512], U8, name="ds_%d" % i, align_bytes=64)
            nc.vector.quantize_mx(
                out=ct[:].bitcast(FP8X4),
                scales=st[:],
                in_=dec_grp[i][:].rearrange("p n w j -> p (n w j)"),
            )
            dec_codes.append((ct, st))

        decb = keep.tile([P, SAMPLES, MODELS], BF16, name="decb")
        decb_bank = []

        def spread_bias():
            bank = psum.tile([P, SAMPLES, MODELS], BF16, name="tr")
            for q in (0, 64):
                nc.tensor.matmul(
                    out=bank[:, q : q + 64, :],
                    lhsT=ones[:],
                    rhs=decb_row[:, :, q : q + 64].rearrange("p n q -> p q n"),
                    start=True,
                    stop=True,
                )
            decb_bank.append(bank)

        def empty_bias():
            nc.scalar.copy(
                out=decb[:].rearrange("p q n -> p (q n)"), in_=decb_bank[0][:].rearrange("p q n -> p (q n)")
            )

        h_bank = {}
        h_grp = {}
        h_codes = []

        def transpose_h(n):
            bank = psum.tile([P, PATCHES, 2, P], F32, name="tr")
            words = h_raw[n // 2][:, n % 2, :].bitcast(F32)
            for l in range(PATCHES):
                for u in range(2):
                    nc.tensor.transpose(bank[:, l, u, :], words[:, 256 * l + u : 256 * (l + 1) : 2], ident[:])
            h_bank[n] = bank

        def empty_h(n):
            if n % 2 == 0:
                gt = keep.tile([P, 2, PATCHES, P, 4], BF16, name="h_grp_%d" % (n // 2), align_bytes=64)
                h_grp[n // 2] = gt
            dst = h_grp[n // 2][:, n % 2, :, :, :].rearrange("p l r j -> p (l r j)").bitcast(F32)
            nc.scalar.copy(
                out=dst.rearrange("p (l r u) -> p l r u", l=PATCHES, u=2),
                in_=h_bank[n][:].rearrange("p l u r -> p l r u"),
            )

        def quantize_h(i):
            ct = keep.tile([P, 512], U32, name="hc_%d" % i, align_bytes=64)
            st = keep.tile([P, 512], U8, name="hs_%d" % i, align_bytes=64)
            nc.vector.quantize_mx(
                out=ct[:].bitcast(FP8X4),
                scales=st[:],
                in_=h_grp[i][:].rearrange("p n l r j -> p (n l r j)"),
            )
            h_codes.append((ct, st))

        r_bank = {}

        def decode(n):
            hc, hs = h_codes[n // 2]
            dc, ds = dec_codes[n // 4]
            for g in range(PASSES):
                if n == 0:
                    bank = psum.tile([P, MODELS, 64], F32, name="acc", bufs=5)
                    r_bank[g] = bank
                a = ((n % 2) * PATCHES + g // 2) * P
                b = (n % 4) * SAMPLES + (g % 2) * 64
                nc.tensor.matmul_mx(
                    out=r_bank[g][:, n, :],
                    lhsT=hc[:, a : a + P].bitcast(FP8X4),
                    lhsT_scale=hs[:, a : a + P],
                    rhs=dc[:, b : b + 64].bitcast(FP8X4),
                    rhs_scale=ds[:, b : b + 64],
                    start=True,
                    stop=True,
                )

        x_rows = {}
        x_bank = {}
        x_grp = {}

        def empty_r(g):
            xt = keep.tile([P, 64, MODELS], BF16, name="x_rows_%d" % g, align_bytes=64)
            nc.vector.tensor_tensor(
                out=xt[:],
                in0=r_bank[g][:].rearrange("p n q -> p q n"),
                in1=decb[:, 64 * (g % 2) : 64 * (g % 2) + 64, :],
                op=ADD,
            )
            x_rows[g] = xt

        def transpose_x(i):
            bank = psum.tile([P, 2, 2, P], F32, name="tr")
            for v in range(2):
                words = x_rows[2 * i + v][:].rearrange("p q n -> p (q n)").bitcast(F32)
                for u in range(2):
                    nc.tensor.transpose(bank[:, v, u, :], words[:, u:256:2], ident[:])
            x_bank[i] = bank

        def empty_x(i):
            xg = keep.tile([P, 2, P, 4], BF16, name="x_grp_%d" % i, align_bytes=64)
            dst = xg[:].rearrange("p v r j -> p (v r j)").bitcast(F32)
            nc.scalar.copy(
                out=dst.rearrange("p (v r u) -> p v r u", v=2, u=2),
                in_=x_bank[i][:].rearrange("p v u r -> p v r u"),
            )
            x_grp[i] = xg

        def quantize_x(i):
            ct = keep.tile([P, 256], U32, name="xc_%d" % i, align_bytes=64)
            st = keep.tile([P, 256], U8, name="xs_%d" % i, align_bytes=64)
            nc.vector.quantize_mx(
                out=ct[:].bitcast(FP8X4),
                scales=st[:],
                in_=x_grp[i][:].rearrange("p v r j -> p (v r j)"),
            )
            x_codes[i] = (ct, st)

        for lo, j in ((0, 1), (1024, 1), (1024, 2), (1024, 3)):
            widen_scalar(0, j, lo, lo + 1024)
        for lo, j in ((0, 0), (1024, 0), (0, 2), (0, 3)):
            widen_vector(0, j, lo, lo + 1024)
        group(0, 0, 1024)
        widen(1, 0, 1024)
        group(0, 1024, 2048)
        flush()
        for i in range(2):
            interleave_dec(i)
        for i in range(2):
            quantize_dec(i)
        spread_bias()
        for n in range(MODELS):
            transpose_h(n)
            if n % 2 == 0 and n // 2 not in (2, 3):
                widen_scalar(1, n // 2, 1024, 2048)
            if n == 1:
                empty_bias()
            empty_h(n)
        for j in (2, 3):
            widen_vector(1, j, 1024, 2048)
        group(1, 0, 1024)
        group(1, 1024, 2048)
        for i in range(4):
            quantize_h(i)
        for n in range(MODELS):
            decode(n)
        widen(2, 0, 1024)
        flush()
        group(2, 0, 1024)
        for g in range(PASSES):
            empty_r(g)

        for i in range(2):
            transpose_x(i)
        widen(2, 1024, 2048)
        for lo in PE_CUTS:
            shuffle_map(2, lo, lo + 256)
        for j in range(4):
            widen_scalar(3, j, 0, 1024)
            if j in (1, 2):
                empty_x(j - 1)
        flush()
        group(2, 1024, 1536)
        for i in range(2):
            quantize_x(i)
        x_ready.append(True)

        group(3, 0, 1024)

        widen(3, 1024, 1536)
        group(3, 1024, 1536)
        widen(3, 1536, 1792)
        empty_map(2, PE_CUTS[0])
        group(3, 1536, 1792)
        widen(3, 1792, 2048)
        empty_map(2, PE_CUTS[1])
        group(3, 1792, 2048)
        finish(0, 512)
        finish(512, 1024)
        flush()
        for lo in PE_CUTS:
            pending.append((2, lo, lo + 256))
            flush()
        for a, b in CUTS[2:]:
            finish(a, b)
